import numpy as np
import ml_dtypes


BF16 = ml_dtypes.bfloat16


def bf(x):
    return np.asarray(x, np.float32).astype(BF16)


def f64(x):
    return np.asarray(x).astype(np.float64)


E2M1 = np.array([0.0, 0.5, 1.0, 1.5, 2.0, 3.0, 4.0, 6.0, -0.0, -0.5, -1.0, -1.5, -2.0, -3.0, -4.0, -6.0])


def pack_weight(w, fmt):
    k, n = w.shape
    w = f64(bf(w)).reshape(k // 32, 32, n)
    amax = np.abs(w).max(1)
    if fmt == "e4m3":
        byte = np.frexp(amax)[1] - 1 + 127 - 7
    else:
        mant, ex = np.frexp(amax / 6.0)
        byte = np.where(mant > 0.5, ex, ex - 1) + 127
    byte = np.clip(np.where(amax > 0, byte, 1), 1, 254)
    scaled = (w * np.exp2(127.0 - byte)[:, None, :]).reshape(k, n).astype(np.float32)
    by_word = np.ascontiguousarray(scaled.reshape(k // 512, 128, 4, n).transpose(0, 1, 3, 2))
    if fmt == "e4m3":
        words = by_word.astype(ml_dtypes.float8_e4m3fn).view(np.uint8)
    else:
        c = by_word.astype(ml_dtypes.float4_e2m1fn).view(np.uint8) & 0xF
        words = c[..., 0::2] | (c[..., 1::2] << 4)
    return np.ascontiguousarray(words), np.ascontiguousarray(byte.astype(np.uint8).reshape(k // 512, 16, n))


def unpack_weight(words, scales, fmt):
    g, p, n, _ = words.shape
    if fmt == "e4m3":
        vals = np.ascontiguousarray(words).view(ml_dtypes.float8_e4m3fn).astype(np.float64)
    else:
        nib = np.empty((g, p, n, 4), np.uint8)
        nib[..., 0::2] = words & 0xF
        nib[..., 1::2] = words >> 4
        vals = E2M1[nib]
    vals = vals * np.repeat(np.exp2(scales.astype(np.float64) - 127.0), 8, axis=1)[..., None]
    return vals.transpose(0, 1, 3, 2).reshape(g * 512, n)

def pack4(w):
    words, scales = pack_weight(w, "e2m1")
    return words.reshape(words.shape[0], 128, -1), scales


def unpack4(words, scales):
    return unpack_weight(words.reshape(words.shape[0], 128, -1, 2), scales, "e2m1")


def kspread(k):
    return np.exp2(np.repeat(np.random.randint(-6, 7, k // 32), 32).astype(np.float64))


B, D_IN, D_H, W_RANK, U_RANK = 512, 2048, 4096, 1024, 1024


def sigmoid(v):
    return 1.0 / (1.0 + np.exp(-v))


def setup_inputs():
    s, t = kspread(W_RANK), kspread(U_RANK)
    wx_r = np.random.standard_normal((B, W_RANK)) * s
    uh_r = np.random.standard_normal((B, U_RANK)) * t
    state = bf(np.random.standard_normal((B, D_H)))
    W2 = np.random.standard_normal((D_H, W_RANK)) * 0.7 / np.sqrt(W_RANK) / s
    U2 = np.random.standard_normal((D_H, U_RANK)) * 0.7 / np.sqrt(U_RANK) / t
    wx_r_words, wx_r_scales = pack4(np.ascontiguousarray(wx_r.T))
    uh_r_words, uh_r_scales = pack4(np.ascontiguousarray(uh_r.T))
    W2_words, W2_scales = pack4(np.ascontiguousarray(W2.T))
    U2_words, U2_scales = pack4(np.ascontiguousarray(U2.T))
    return {
        "wx_r_words": wx_r_words,
        "wx_r_scales": wx_r_scales,
        "uh_r_words": uh_r_words,
        "uh_r_scales": uh_r_scales,
        "state": state,
        "W2_words": W2_words,
        "W2_scales": W2_scales,
        "U2_words": U2_words,
        "U2_scales": U2_scales,
        "bias_gate": bf(1.0 + 0.5 * np.random.standard_normal((1, D_H))),
        "bias_update": bf(1.0 + 0.5 * np.random.standard_normal((1, D_H))),
        "zeta": bf(1.0 + 0.1 * np.random.standard_normal((1, 1))),
        "nu": bf(-1.5 + 0.1 * np.random.standard_normal((1, 1))),
    }


def reference(wx_r_words, wx_r_scales, uh_r_words, uh_r_scales, state, W2_words, W2_scales, U2_words, U2_scales, bias_gate, bias_update, zeta, nu):
    wx = unpack4(wx_r_words, wx_r_scales).T @ unpack4(W2_words, W2_scales)
    uh = unpack4(uh_r_words, uh_r_scales).T @ unpack4(U2_words, U2_scales)
    pre = wx + uh
    z = sigmoid(pre + f64(bias_gate))
    h_cand = np.tanh(pre + f64(bias_update))
    return z * f64(state) + (sigmoid(f64(zeta)) * (1.0 - z) + sigmoid(f64(nu))) * h_cand

@@ -1,0 +1,258 @@
+from contextlib import ExitStack
+
+import concourse.mybir as mybir
+from concourse.masks import make_identity
+
+F32 = mybir.dt.float32
+BF16 = mybir.dt.bfloat16
+U8 = mybir.dt.uint8
+I32 = mybir.dt.int32
+FP4X4 = mybir.dt.float4_e2m1fn_x4
+ACT = mybir.ActivationFunctionType
+ALU = mybir.AluOpType
+
+B, D_H, RANK = 512, 4096, 1024
+FLOPS = 2 * B * D_H * 2 * RANK
+
+P = 128
+NBB = B // P
+NBLK = D_H // P
+CHUNK = 512
+NCH = D_H // CHUNK
+SC_RANGES = ((0, 512), (512, 2048), (2048, 4096))
+UNITS = tuple((2 * i, 2) for i in range(15)) + ((30, 1), (31, 1))
+NU = len(UNITS)
+LAG = 2
+WARM = 6
+V_EVAC = (14, 15, 16)
+
+
+def tile_fastgrnncudacell_pa_kernel(
+    tc,
+    wx_r_words,
+    wx_r_scales,
+    uh_r_words,
+    uh_r_scales,
+    state,
+    W2_words,
+    W2_scales,
+    U2_words,
+    U2_scales,
+    bias_gate,
+    bias_update,
+    zeta,
+    nu,
+    out,
+):
+    nc = tc.nc
+    x_words = (wx_r_words, uh_r_words)
+    x_scales = (wx_r_scales, uh_r_scales)
+    w_words = (W2_words, U2_words)
+    w_scales = (W2_scales, U2_scales)
+    with ExitStack() as ctx:
+        ctx.enter_context(tc.manual_schedule())
+        keep = ctx.enter_context(tc.tile_pool(name="keep", bufs=1))
+        work = ctx.enter_context(tc.tile_pool(name="work", bufs=3))
+        psum = ctx.enter_context(tc.psum_pool(name="psum", bufs=2))
+
+        state_v = state.rearrange("(b p) c -> p b c", p=P)
+        out_v = out.rearrange("(b p) c -> p b c", p=P)
+
+        xc = [keep.tile([P, 2, 2 * B], U8, name="xc%d" % a, align_bytes=64) for a in range(2)]
+        xs = [keep.tile([P, 2, B], U8, name="xs%d" % a, align_bytes=64) for a in range(2)]
+        ws = [
+            [keep.tile([P, 2, c1 - c0], U8, name="ws%d_%d" % (a, i), align_bytes=64) for i, (c0, c1) in enumerate(SC_RANGES)]
+            for a in range(2)
+        ]
+        wc = [[keep.tile([P, 2, 2 * CHUNK], U8, name="wc%d_%d" % (a, k), align_bytes=64) for k in range(NCH)] for a in range(2)]
+        st = [keep.tile([P, NBB, CHUNK], BF16, name="st%d" % k) for k in range(NCH)]
+        ident_bf = keep.tile([P, P], BF16, name="ident_bf")
+        ident_f = keep.tile([P, P], F32, name="ident_f")
+        braw = keep.tile([P, P], BF16, name="braw")
+        bias_sb = keep.tile([P, 2 * NBLK], F32, name="bias_sb")
+        zt = keep.tile([P, 1], BF16, name="zt")
+        nt = keep.tile([P, 1], BF16, name="nt")
+        warm = keep.tile([P, 1], F32, name="warm")
+        warm2 = keep.tile([P, 1], F32, name="warm2")
+        sz = keep.tile([P, 1], F32, name="sz")
+        sn = keep.tile([P, 1], F32, name="sn")
+        nsz = keep.tile([P, 1], F32, name="nsz")
+        amix = keep.tile([P, 1], F32, name="amix")
+        zeros = keep.tile([P, B], BF16, name="zeros")
+
+        nc.vector.memset(xs[0][:].bitcast(I32), 0)
+        nc.vector.memset(ws[0][0][:].bitcast(I32), 0)
+        nc.vector.memset(xs[1][:].bitcast(I32), 0)
+        nc.vector.memset(ws[1][0][:].bitcast(I32), 0)
+        nc.vector.memset(warm[:], 0.0)
+        nc.vector.memset(zeros[:], 0.0)
+        nc.vector.memset(braw[64:128, :], 0.0)
+        for i in (1, 2):
+            for a in range(2):
+                nc.vector.memset(ws[a][i][:].bitcast(I32), 0)
+
+        nc.gpsimd.dma_start(out=braw[0:32, :], in_=bias_gate.rearrange("o (j p) -> (o j) p", p=P))
+        nc.gpsimd.dma_start(out=braw[32:64, :], in_=bias_update.rearrange("o (j p) -> (o j) p", p=P))
+        make_identity(nc, ident_bf[:])
+        nc.gpsimd.dma_start(out=zt[:], in_=zeta.rearrange("a b -> (a b)").partition_broadcast(P))
+        nc.gpsimd.dma_start(out=nt[:], in_=nu.rearrange("a b -> (a b)").partition_broadcast(P))
+        make_identity(nc, ident_f[:])
+
+        nc.scalar.activation(out=warm2[:], in_=warm[:], func=ACT.Sigmoid)
+
+        def load_scales(plane, dram, c0, c1):
+            for quad in range(4):
+                nc.sync.dma_start(
+                    out=plane[32 * quad : 32 * quad + 4, :, :].bitcast(I32),
+                    in_=dram[:, 4 * quad : 4 * quad + 4, c0:c1].rearrange("g r n -> r g n").bitcast(I32),
+                )
+
+        def load_codes(tile_ap, dram, b0, b1):
+            nc.sync.dma_start(
+                out=tile_ap[:].bitcast(I32), in_=dram[:, :, b0:b1].rearrange("g p n -> p g n").bitcast(I32)
+            )
+
+        def load_state(k):
+            nc.sync.dma_start(out=st[k][:], in_=state_v[:, :, CHUNK * k : CHUNK * (k + 1)])
+
+        for a in range(2):
+            load_scales(xs[a], x_scales[a], 0, B)
+            load_scales(ws[a][0], w_scales[a], 0, SC_RANGES[0][1])
+            load_codes(xc[a], x_words[a], 0, 2 * B)
+            load_codes(wc[a][0], w_words[a], 0, 2 * CHUNK)
+        load_state(0)
+        for i in (1, 2):
+            c0, c1 = SC_RANGES[i]
+            for a in range(2):
+                load_scales(ws[a][i], w_scales[a], c0, c1)
+            for k in range(c0 // CHUNK, c1 // CHUNK):
+                for a in range(2):
+                    load_codes(wc[a][k], w_words[a], 2 * CHUNK * k, 2 * CHUNK * (k + 1))
+                load_state(k)
+
+        for i in range(WARM):
+            dummy = psum.tile([P, B], F32, tag="oT", bufs=2, name="dummy")
+            nc.tensor.matmul(out=dummy[:], lhsT=zeros[:, 0:P], rhs=zeros[:], start=True, stop=True)
+
+        def scale_plane(a, j):
+            ch = P * j
+            for i, (c0, c1) in enumerate(SC_RANGES):
+                if c0 <= ch < c1:
+                    return ws[a][i], ch - c0
+            raise ValueError("no range")
+
+        pres = {}
+        sts = {}
+        cs = {}
+        zs = {}
+        outs = {}
+        oTs = {}
+
+        def mx_block(j, passes):
+            k, jl = j // 4, j % 4
+            if j not in pres:
+                pres[j] = psum.tile([P, B], F32, tag="pre", bufs=4, name="pre")
+            for q in passes:
+                a, g = q // 2, q % 2
+                plane, col = scale_plane(a, j)
+                nc.tensor.matmul_mx(
+                    out=pres[j][:],
+                    lhsT=wc[a][k][:, g, 2 * P * jl : 2 * P * (jl + 1)].bitcast(FP4X4),
+                    lhsT_scale=plane[:, g, col : col + P],
+                    rhs=xc[a][:, g, :].bitcast(FP4X4),
+                    rhs_scale=xs[a][:, g, :],
+                    start=(q == 0),
+                    stop=(q == 3),
+                )
+
+        def state_t(u):
+            j0, nb = UNITS[u]
+            stT = psum.tile([P, nb, B], BF16, tag="stT", bufs=2, name="stT")
+            for jj in range(nb):
+                k, jl = (j0 + jj) // 4, (j0 + jj) % 4
+                for bb in range(NBB):
+                    nc.tensor.transpose(
+                        stT[:, jj, P * bb : P * (bb + 1)], st[k][:, bb, P * jl : P * (jl + 1)], ident_bf[:]
+                    )
+            sts[u] = stT
+
+        def act(u):
+            j0, nb = UNITS[u]
+            c = work.tile([P, nb, B], F32, tag="c", name="c")
+            z = work.tile([P, nb, B], F32, tag="z", name="z")
+            for jj in range(nb):
+                j = j0 + jj
+                nc.scalar.activation(
+                    out=c[:, jj, :], in_=pres[j][:], func=ACT.Tanh, bias=bias_sb[:, NBLK + j : NBLK + j + 1]
+                )
+            for jj in range(nb):
+                j = j0 + jj
+                nc.scalar.activation(out=z[:, jj, :], in_=pres[j][:], func=ACT.Sigmoid, bias=bias_sb[:, j : j + 1])
+            cs[u] = c
+            zs[u] = z
+
+        def mix(u):
+            j0, nb = UNITS[u]
+            t1 = work.tile([P, nb, B], F32, tag="t1", name="t1")
+            t2 = work.tile([P, nb, B], F32, tag="t2", name="t2")
+            o = work.tile([P, nb, B], F32, tag="o", bufs=4, name="o")
+            nc.vector.scalar_tensor_tensor(
+                out=t1[:], in0=cs[u][:], scalar=nsz[:, 0:1], in1=sts[u][:], op0=ALU.mult, op1=ALU.add
+            )
+            nc.vector.tensor_tensor(out=t2[:], in0=t1[:], in1=zs[u][:], op=ALU.mult)
+            nc.vector.scalar_tensor_tensor(
+                out=o[:], in0=cs[u][:], scalar=amix[:, 0:1], in1=t2[:], op0=ALU.mult, op1=ALU.add
+            )
+            outs[u] = o
+
+        def out_t(u):
+            j0, nb = UNITS[u]
+            halves = []
+            for h in range(2):
+                oT = psum.tile([P, 2, nb * P], F32, tag="oT", bufs=2, name="oT")
+                for b2 in range(2):
+                    bb = 2 * h + b2
+                    for jj in range(nb):
+                        nc.tensor.transpose(
+                            oT[:, b2, P * jj : P * (jj + 1)], outs[u][:, jj, P * bb : P * (bb + 1)], ident_f[:]
+                        )
+                halves.append(oT)
+            oTs[u] = halves
+
+        def evac(u):
+            j0, nb = UNITS[u]
+            osb = work.tile([P, NBB, nb * P], F32, tag="osb", bufs=4, name="osb")
+            for h in range(2):
+                if h == 1 and u in V_EVAC:
+                    nc.vector.tensor_copy(out=osb[:, 2 * h : 2 * h + 2, :], in_=oTs[u][h][:])
+                else:
+                    nc.scalar.copy(out=osb[:, 2 * h : 2 * h + 2, :], in_=oTs[u][h][:])
+            nc.sync.dma_start(out=out_v[:, :, P * j0 : P * (j0 + nb)], in_=osb[:])
+
+        for j in range(4):
+            mx_block(j, (0, 1))
+        bT = psum.tile([P, P], BF16, tag="stT", bufs=2, name="bT")
+        nc.tensor.transpose(bT[:], braw[:], ident_bf[:])
+        nc.vector.tensor_copy(out=bias_sb[:], in_=bT[:, 0 : 2 * NBLK])
+        nc.scalar.activation(out=sz[:], in_=zt[:], func=ACT.Sigmoid)
+        nc.scalar.activation(out=sn[:], in_=nt[:], func=ACT.Sigmoid)
+        nc.vector.tensor_scalar_mul(out=nsz[:], in0=sz[:], scalar1=-1.0)
+        nc.vector.tensor_add(out=amix[:], in0=sz[:], in1=sn[:])
+        for j in range(4):
+            mx_block(j, (2, 3))
+
+        for s in range(NU + LAG):
+            if s < NU:
+                j0, nb = UNITS[s]
+                if j0 >= 4:
+                    for jj in range(nb):
+                        mx_block(j0 + jj, (0, 1, 2, 3))
+                state_t(s)
+            if s >= LAG:
+                out_t(s - LAG)
+            if s < NU:
+                act(s)
+            if s >= LAG:
+                evac(s - LAG)
+            if s < NU:
+                mix(s)

@@ -20,10 +20,12 @@ NBLK = D_H // P
 CHUNK = 512
 NCH = D_H // CHUNK
 SC_RANGES = ((0, 512), (512, 2048), (2048, 4096))
+SC_RANGES = ((0, 1024), (1024, 2560), (2560, 4096))
+RANGE_BEFORE = {2: 1, 4: 2}
 UNITS = tuple((2 * i, 2) for i in range(15)) + ((30, 1), (31, 1))
 NU = len(UNITS)
 LAG = 2
-WARM = 6
+WARM = 14
 V_EVAC = (14, 15, 16)
 
 
@@ -121,14 +123,14 @@ def tile_fastgrnncudacell_pa_kernel(
             load_codes(xc[a], x_words[a], 0, 2 * B)
             load_codes(wc[a][0], w_words[a], 0, 2 * CHUNK)
         load_state(0)
-        for i in (1, 2):
-            c0, c1 = SC_RANGES[i]
-            for a in range(2):
-                load_scales(ws[a][i], w_scales[a], c0, c1)
-            for k in range(c0 // CHUNK, c1 // CHUNK):
+        for k in range(1, NCH):
+            if k in RANGE_BEFORE:
+                i = RANGE_BEFORE[k]
                 for a in range(2):
-                    load_codes(wc[a][k], w_words[a], 2 * CHUNK * k, 2 * CHUNK * (k + 1))
-                load_state(k)
+                    load_scales(ws[a][i], w_scales[a], SC_RANGES[i][0], SC_RANGES[i][1])
+            for a in range(2):
+                load_codes(wc[a][k], w_words[a], 2 * CHUNK * k, 2 * CHUNK * (k + 1))
+            load_state(k)
 
         for i in range(WARM):
             dummy = psum.tile([P, B], F32, tag="oT", bufs=2, name="dummy")
@@ -191,19 +193,27 @@ def tile_fastgrnncudacell_pa_kernel(
             cs[u] = c
             zs[u] = z
 
-        def mix(u):
+        t1s = {}
+        t2s = {}
+
+        def v3(u):
             j0, nb = UNITS[u]
-            t1 = work.tile([P, nb, B], F32, tag="t1", name="t1")
-            t2 = work.tile([P, nb, B], F32, tag="t2", name="t2")
-            o = work.tile([P, nb, B], F32, tag="o", bufs=4, name="o")
+            t1s[u] = work.tile([P, nb, B], F32, tag="t1", name="t1")
             nc.vector.scalar_tensor_tensor(
-                out=t1[:], in0=cs[u][:], scalar=nsz[:, 0:1], in1=sts[u][:], op0=ALU.mult, op1=ALU.add
+                out=t1s[u][:], in0=cs[u][:], scalar=nsz[:, 0:1], in1=sts[u][:], op0=ALU.mult, op1=ALU.add
             )
-            nc.vector.tensor_tensor(out=t2[:], in0=t1[:], in1=zs[u][:], op=ALU.mult)
+
+        def v4(u):
+            j0, nb = UNITS[u]
+            t2s[u] = work.tile([P, nb, B], F32, tag="t2", name="t2")
+            nc.vector.tensor_tensor(out=t2s[u][:], in0=t1s[u][:], in1=zs[u][:], op=ALU.mult)
+
+        def v5(u):
+            j0, nb = UNITS[u]
+            outs[u] = work.tile([P, nb, B], F32, tag="o", bufs=4, name="o")
             nc.vector.scalar_tensor_tensor(
-                out=o[:], in0=cs[u][:], scalar=amix[:, 0:1], in1=t2[:], op0=ALU.mult, op1=ALU.add
+                out=outs[u][:], in0=cs[u][:], scalar=amix[:, 0:1], in1=t2s[u][:], op0=ALU.mult, op1=ALU.add
             )
-            outs[u] = o
 
         def out_t(u):
             j0, nb = UNITS[u]
@@ -255,4 +265,8 @@ def tile_fastgrnncudacell_pa_kernel(
             if s >= LAG:
                 evac(s - LAG)
             if s < NU:
-                mix(s)
+                v3(s)
+            if 1 <= s <= NU:
+                v5(s - 1)
+            if s < NU:
+                v4(s)

@@ -27,6 +27,7 @@ NU = len(UNITS)
 LAG = 2
 WARM = 14
 V_EVAC = (14, 15, 16)
+OSB_BUFS = 10
 
 
 def tile_fastgrnncudacell_pa_kernel(
@@ -231,7 +232,7 @@ def tile_fastgrnncudacell_pa_kernel(
 
         def evac(u):
             j0, nb = UNITS[u]
-            osb = work.tile([P, NBB, nb * P], F32, tag="osb", bufs=4, name="osb")
+            osb = work.tile([P, NBB, nb * P], F32, tag="osb", bufs=OSB_BUFS, name="osb")
             for h in range(2):
                 if h == 1 and u in V_EVAC:
                     nc.vector.tensor_copy(out=osb[:, 2 * h : 2 * h + 2, :], in_=oTs[u][h][:])

@@ -22,12 +22,12 @@ NCH = D_H // CHUNK
 SC_RANGES = ((0, 512), (512, 2048), (2048, 4096))
 SC_RANGES = ((0, 1024), (1024, 2560), (2560, 4096))
 RANGE_BEFORE = {2: 1, 4: 2}
-UNITS = tuple((2 * i, 2) for i in range(15)) + ((30, 1), (31, 1))
+KB = 1
+UNITS = (("A", 0, 2), ("A", 2, 2)) + tuple(("A", 2 * i, 2) for i in range(4, 15)) + (("A", 30, 1), ("A", 31, 1))
 NU = len(UNITS)
-LAG = 2
+B_AT = {2: 0, 5: 1, 8: 2, 11: 3}
 WARM = 14
-V_EVAC = (14, 15, 16)
-OSB_BUFS = 10
+V_EVAC = (NU - 1,)
 
 
 def tile_fastgrnncudacell_pa_kernel(
@@ -82,6 +82,8 @@ def tile_fastgrnncudacell_pa_kernel(
         nsz = keep.tile([P, 1], F32, name="nsz")
         amix = keep.tile([P, 1], F32, name="amix")
         zeros = keep.tile([P, B], BF16, name="zeros")
+        bgB = keep.tile([P, CHUNK], BF16, name="bgB")
+        buB = keep.tile([P, CHUNK], BF16, name="buB")
 
         nc.vector.memset(xs[0][:].bitcast(I32), 0)
         nc.vector.memset(ws[0][0][:].bitcast(I32), 0)
@@ -132,6 +134,13 @@ def tile_fastgrnncudacell_pa_kernel(
             for a in range(2):
                 load_codes(wc[a][k], w_words[a], 2 * CHUNK * k, 2 * CHUNK * (k + 1))
             load_state(k)
+            if k == KB:
+                nc.sync.dma_start(
+                    out=bgB[:], in_=bias_gate[:, CHUNK * KB : CHUNK * (KB + 1)].rearrange("o n -> (o n)").partition_broadcast(P)
+                )
+                nc.sync.dma_start(
+                    out=buB[:], in_=bias_update[:, CHUNK * KB : CHUNK * (KB + 1)].rearrange("o n -> (o n)").partition_broadcast(P)
+                )
 
         for i in range(WARM):
             dummy = psum.tile([P, B], F32, tag="oT", bufs=2, name="dummy")
@@ -169,7 +178,7 @@ def tile_fastgrnncudacell_pa_kernel(
                 )
 
         def state_t(u):
-            j0, nb = UNITS[u]
+            kind, j0, nb = UNITS[u]
             stT = psum.tile([P, nb, B], BF16, tag="stT", bufs=2, name="stT")
             for jj in range(nb):
                 k, jl = (j0 + jj) // 4, (j0 + jj) % 4
@@ -180,7 +189,7 @@ def tile_fastgrnncudacell_pa_kernel(
             sts[u] = stT
 
         def act(u):
-            j0, nb = UNITS[u]
+            kind, j0, nb = UNITS[u]
             c = work.tile([P, nb, B], F32, tag="c", name="c")
             z = work.tile([P, nb, B], F32, tag="z", name="z")
             for jj in range(nb):
@@ -198,26 +207,26 @@ def tile_fastgrnncudacell_pa_kernel(
         t2s = {}
 
         def v3(u):
-            j0, nb = UNITS[u]
+            kind, j0, nb = UNITS[u]
             t1s[u] = work.tile([P, nb, B], F32, tag="t1", name="t1")
             nc.vector.scalar_tensor_tensor(
                 out=t1s[u][:], in0=cs[u][:], scalar=nsz[:, 0:1], in1=sts[u][:], op0=ALU.mult, op1=ALU.add
             )
 
         def v4(u):
-            j0, nb = UNITS[u]
+            kind, j0, nb = UNITS[u]
             t2s[u] = work.tile([P, nb, B], F32, tag="t2", name="t2")
             nc.vector.tensor_tensor(out=t2s[u][:], in0=t1s[u][:], in1=zs[u][:], op=ALU.mult)
 
         def v5(u):
-            j0, nb = UNITS[u]
+            kind, j0, nb = UNITS[u]
             outs[u] = work.tile([P, nb, B], F32, tag="o", bufs=4, name="o")
             nc.vector.scalar_tensor_tensor(
                 out=outs[u][:], in0=cs[u][:], scalar=amix[:, 0:1], in1=t2s[u][:], op0=ALU.mult, op1=ALU.add
             )
 
         def out_t(u):
-            j0, nb = UNITS[u]
+            kind, j0, nb = UNITS[u]
             halves = []
             for h in range(2):
                 oT = psum.tile([P, 2, nb * P], F32, tag="oT", bufs=2, name="oT")
@@ -231,14 +240,71 @@ def tile_fastgrnncudacell_pa_kernel(
             oTs[u] = halves
 
         def evac(u):
-            j0, nb = UNITS[u]
-            osb = work.tile([P, NBB, nb * P], F32, tag="osb", bufs=OSB_BUFS, name="osb")
+            kind, j0, nb = UNITS[u]
+            osb = work.tile([P, NBB, nb * P], F32, tag="osb", bufs=4, name="osb")
             for h in range(2):
                 if h == 1 and u in V_EVAC:
                     nc.vector.tensor_copy(out=osb[:, 2 * h : 2 * h + 2, :], in_=oTs[u][h][:])
                 else:
                     nc.scalar.copy(out=osb[:, 2 * h : 2 * h + 2, :], in_=oTs[u][h][:])
             nc.sync.dma_start(out=out_v[:, :, P * j0 : P * (j0 + nb)], in_=osb[:])
+
+        avs = {}
+        bvs = {}
+
+        def mx_b(u):
+            bb = u
+            pre = psum.tile([P, CHUNK], F32, tag="pre", bufs=4, name="pre")
+            for q in range(4):
+                a, g = q // 2, q % 2
+                plane, col = scale_plane(a, 4 * KB)
+                nc.tensor.matmul_mx(
+                    out=pre[:],
+                    lhsT=xc[a][:, g, 2 * P * bb : 2 * P * (bb + 1)].bitcast(FP4X4),
+                    lhsT_scale=xs[a][:, g, P * bb : P * (bb + 1)],
+                    rhs=wc[a][KB][:, g, :].bitcast(FP4X4),
+                    rhs_scale=plane[:, g, col : col + CHUNK],
+                    start=(q == 0),
+                    stop=(q == 3),
+                )
+            pres[("B", bb)] = pre
+
+        def v12_b(u):
+            bb = u
+            avs[("B", u)] = work.tile([P, CHUNK], F32, tag="av", bufs=2, name="av")
+            bvs[("B", u)] = work.tile([P, CHUNK], F32, tag="bv", bufs=2, name="bv")
+            nc.vector.tensor_tensor(out=bvs[("B", u)][:], in0=pres[("B", bb)][:], in1=buB[:], op=ALU.add)
+            nc.vector.tensor_tensor(out=avs[("B", u)][:], in0=pres[("B", bb)][:], in1=bgB[:], op=ALU.add)
+
+        def act_b(u):
+            cs[("B", u)] = work.tile([P, CHUNK], F32, tag="cB", bufs=2, name="cB")
+            zs[("B", u)] = work.tile([P, CHUNK], F32, tag="zB", bufs=2, name="zB")
+            nc.scalar.activation(out=cs[("B", u)][:], in_=bvs[("B", u)][:], func=ACT.Tanh)
+            nc.scalar.activation(out=zs[("B", u)][:], in_=avs[("B", u)][:], func=ACT.Sigmoid)
+
+        def v3_b(u):
+            bb = u
+            t1s[("B", u)] = work.tile([P, CHUNK], F32, tag="t1B", bufs=2, name="t1B")
+            nc.vector.scalar_tensor_tensor(
+                out=t1s[("B", u)][:], in0=cs[("B", u)][:], scalar=nsz[:, 0:1], in1=st[KB][:, bb, :], op0=ALU.mult, op1=ALU.add
+            )
+
+        def v4_b(u):
+            t2s[("B", u)] = work.tile([P, CHUNK], F32, tag="t2B", bufs=2, name="t2B")
+            nc.vector.tensor_tensor(out=t2s[("B", u)][:], in0=t1s[("B", u)][:], in1=zs[("B", u)][:], op=ALU.mult)
+
+        def v5_b(u):
+            bb = u
+            ob = work.tile([P, CHUNK], F32, tag="ob", bufs=2, name="ob")
+            nc.vector.scalar_tensor_tensor(
+                out=ob[:], in0=cs[("B", u)][:], scalar=amix[:, 0:1], in1=t2s[("B", u)][:], op0=ALU.mult, op1=ALU.add
+            )
+            nc.sync.dma_start(out=out[P * bb : P * (bb + 1), CHUNK * KB : CHUNK * (KB + 1)], in_=ob[:])
+
+        def kind_of(u):
+            if 0 <= u < NU:
+                return UNITS[u][0]
+            return "-"
 
         for j in range(4):
             mx_block(j, (0, 1))
@@ -252,22 +318,39 @@ def tile_fastgrnncudacell_pa_kernel(
         for j in range(4):
             mx_block(j, (2, 3))
 
-        for s in range(NU + LAG):
-            if s < NU:
-                j0, nb = UNITS[s]
+        def b_at(s, lag):
+            return B_AT.get(s - lag, None)
+
+        for s in range(NU + 4):
+            k0, k1, k2 = kind_of(s), kind_of(s - 1), kind_of(s - 2)
+            if k0 == "A":
+                kind, j0, nb = UNITS[s]
                 if j0 >= 4:
                     for jj in range(nb):
                         mx_block(j0 + jj, (0, 1, 2, 3))
+            if b_at(s, 0) is not None:
+                mx_b(b_at(s, 0))
+            if k0 == "A":
                 state_t(s)
-            if s >= LAG:
-                out_t(s - LAG)
-            if s < NU:
+            if k2 == "A":
+                out_t(s - 2)
+            if k0 == "A":
                 act(s)
-            if s >= LAG:
-                evac(s - LAG)
-            if s < NU:
+            if k2 == "A":
+                evac(s - 2)
+            if b_at(s, 1) is not None:
+                act_b(b_at(s, 1))
+            if k0 == "A":
                 v3(s)
-            if 1 <= s <= NU:
+            if b_at(s, 2) is not None:
+                v3_b(b_at(s, 2))
+            if k1 == "A":
                 v5(s - 1)
-            if s < NU:
+            if b_at(s, 3) is not None:
+                v5_b(b_at(s, 3))
+            if k0 == "A":
                 v4(s)
+            if b_at(s, 2) is not None:
+                v4_b(b_at(s, 2))
+            if b_at(s, 0) is not None:
+                v12_b(b_at(s, 0))

@@ -21,11 +21,11 @@ CHUNK = 512
 NCH = D_H // CHUNK
 SC_RANGES = ((0, 512), (512, 2048), (2048, 4096))
 SC_RANGES = ((0, 1024), (1024, 2560), (2560, 4096))
-RANGE_BEFORE = {2: 1, 4: 2}
-KB = 1
-UNITS = (("A", 0, 2), ("A", 2, 2)) + tuple(("A", 2 * i, 2) for i in range(4, 15)) + (("A", 30, 1), ("A", 31, 1))
+LOAD_ORDER = (1, -1, 3, 2, -2, 4, 5, 6, 7)
+KB = 2
+UNITS = tuple(("A", 2 * i, 2) for i in range(4)) + tuple(("A", 2 * i, 2) for i in range(6, 15)) + (("A", 30, 1), ("A", 31, 1))
 NU = len(UNITS)
-B_AT = {2: 0, 5: 1, 8: 2, 11: 3}
+B_AT = {4: 0, 7: 1, 10: 2, 12: 3}
 WARM = 14
 V_EVAC = (NU - 1,)
 
@@ -82,8 +82,10 @@ def tile_fastgrnncudacell_pa_kernel(
         nsz = keep.tile([P, 1], F32, name="nsz")
         amix = keep.tile([P, 1], F32, name="amix")
         zeros = keep.tile([P, B], BF16, name="zeros")
-        bgB = keep.tile([P, CHUNK], BF16, name="bgB")
-        buB = keep.tile([P, CHUNK], BF16, name="buB")
+        bgB = keep.tile([P, CHUNK], F32, name="bgB")
+        buB = keep.tile([P, CHUNK], F32, name="buB")
+        ones = keep.tile([P, P], BF16, name="ones")
+        brow = keep.tile([P, 2, CHUNK], BF16, name="brow")
 
         nc.vector.memset(xs[0][:].bitcast(I32), 0)
         nc.vector.memset(ws[0][0][:].bitcast(I32), 0)
@@ -92,6 +94,8 @@ def tile_fastgrnncudacell_pa_kernel(
         nc.vector.memset(warm[:], 0.0)
         nc.vector.memset(zeros[:], 0.0)
         nc.vector.memset(braw[64:128, :], 0.0)
+        nc.vector.memset(ones[:], 1.0)
+        nc.vector.memset(brow[:], 0.0)
         for i in (1, 2):
             for a in range(2):
                 nc.vector.memset(ws[a][i][:].bitcast(I32), 0)
@@ -102,6 +106,8 @@ def tile_fastgrnncudacell_pa_kernel(
         nc.gpsimd.dma_start(out=zt[:], in_=zeta.rearrange("a b -> (a b)").partition_broadcast(P))
         nc.gpsimd.dma_start(out=nt[:], in_=nu.rearrange("a b -> (a b)").partition_broadcast(P))
         make_identity(nc, ident_f[:])
+        nc.gpsimd.dma_start(out=brow[0:1, 0, :], in_=bias_gate[:, CHUNK * KB : CHUNK * (KB + 1)])
+        nc.gpsimd.dma_start(out=brow[0:1, 1, :], in_=bias_update[:, CHUNK * KB : CHUNK * (KB + 1)])
 
         nc.scalar.activation(out=warm2[:], in_=warm[:], func=ACT.Sigmoid)
 
@@ -126,21 +132,15 @@ def tile_fastgrnncudacell_pa_kernel(
             load_codes(xc[a], x_words[a], 0, 2 * B)
             load_codes(wc[a][0], w_words[a], 0, 2 * CHUNK)
         load_state(0)
-        for k in range(1, NCH):
-            if k in RANGE_BEFORE:
-                i = RANGE_BEFORE[k]
+        for item in LOAD_ORDER:
+            if item < 0:
+                i = -item
                 for a in range(2):
                     load_scales(ws[a][i], w_scales[a], SC_RANGES[i][0], SC_RANGES[i][1])
-            for a in range(2):
-                load_codes(wc[a][k], w_words[a], 2 * CHUNK * k, 2 * CHUNK * (k + 1))
-            load_state(k)
-            if k == KB:
-                nc.sync.dma_start(
-                    out=bgB[:], in_=bias_gate[:, CHUNK * KB : CHUNK * (KB + 1)].rearrange("o n -> (o n)").partition_broadcast(P)
-                )
-                nc.sync.dma_start(
-                    out=buB[:], in_=bias_update[:, CHUNK * KB : CHUNK * (KB + 1)].rearrange("o n -> (o n)").partition_broadcast(P)
-                )
+            else:
+                for a in range(2):
+                    load_codes(wc[a][item], w_words[a], 2 * CHUNK * item, 2 * CHUNK * (item + 1))
+                load_state(item)
 
         for i in range(WARM):
             dummy = psum.tile([P, B], F32, tag="oT", bufs=2, name="dummy")
@@ -338,6 +338,11 @@ def tile_fastgrnncudacell_pa_kernel(
                 act(s)
             if k2 == "A":
                 evac(s - 2)
+            if s == 1:
+                for i, dst in enumerate((bgB, buB)):
+                    pb = psum.tile([P, CHUNK], F32, tag="oT", bufs=2, name="pb")
+                    nc.tensor.matmul(out=pb[:], lhsT=ones[:], rhs=brow[:, i, :], start=True, stop=True)
+                    nc.scalar.copy(out=dst[:], in_=pb[:])
             if b_at(s, 1) is not None:
                 act_b(b_at(s, 1))
             if k0 == "A":

from contextlib import ExitStack

import concourse.mybir as mybir
from concourse.masks import make_identity

F32 = mybir.dt.float32
BF16 = mybir.dt.bfloat16
U8 = mybir.dt.uint8
I32 = mybir.dt.int32
FP4X4 = mybir.dt.float4_e2m1fn_x4
ACT = mybir.ActivationFunctionType
ALU = mybir.AluOpType

B, D_H, RANK = 512, 4096, 1024
FLOPS = 2 * B * D_H * 2 * RANK

P = 128
NBB = B // P
NBLK = D_H // P
CHUNK = 512
NCH = D_H // CHUNK
SC_RANGES = ((0, 512), (512, 2048), (2048, 4096))
SC_RANGES = ((0, 1024), (1024, 2560), (2560, 4096))
LOAD_ORDER = (1, -1, 3, 2, -2, 4, 5, 6, 7)
KB = 2
UNITS = tuple(("A", 2 * i, 2) for i in range(4)) + tuple(("A", 2 * i, 2) for i in range(6, 15)) + (("A", 30, 1), ("A", 31, 1))
NU = len(UNITS)
B_AT = {4: 0, 7: 1, 10: 2, 12: 3}
WARM = 14
V_EVAC = (NU - 1,)


def tile_fastgrnncudacell_pa_kernel(
    tc,
    wx_r_words,
    wx_r_scales,
    uh_r_words,
    uh_r_scales,
    state,
    W2_words,
    W2_scales,
    U2_words,
    U2_scales,
    bias_gate,
    bias_update,
    zeta,
    nu,
    out,
):
    nc = tc.nc
    x_words = (wx_r_words, uh_r_words)
    x_scales = (wx_r_scales, uh_r_scales)
    w_words = (W2_words, U2_words)
    w_scales = (W2_scales, U2_scales)
    with ExitStack() as ctx:
        ctx.enter_context(tc.manual_schedule())
        keep = ctx.enter_context(tc.tile_pool(name="keep", bufs=1))
        work = ctx.enter_context(tc.tile_pool(name="work", bufs=3))
        psum = ctx.enter_context(tc.psum_pool(name="psum", bufs=2))

        state_v = state.rearrange("(b p) c -> p b c", p=P)
        out_v = out.rearrange("(b p) c -> p b c", p=P)

        xc = [keep.tile([P, 2, 2 * B], U8, name="xc%d" % a, align_bytes=64) for a in range(2)]
        xs = [keep.tile([P, 2, B], U8, name="xs%d" % a, align_bytes=64) for a in range(2)]
        ws = [
            [keep.tile([P, 2, c1 - c0], U8, name="ws%d_%d" % (a, i), align_bytes=64) for i, (c0, c1) in enumerate(SC_RANGES)]
            for a in range(2)
        ]
        wc = [[keep.tile([P, 2, 2 * CHUNK], U8, name="wc%d_%d" % (a, k), align_bytes=64) for k in range(NCH)] for a in range(2)]
        st = [keep.tile([P, NBB, CHUNK], BF16, name="st%d" % k) for k in range(NCH)]
        ident_bf = keep.tile([P, P], BF16, name="ident_bf")
        ident_f = keep.tile([P, P], F32, name="ident_f")
        braw = keep.tile([P, P], BF16, name="braw")
        bias_sb = keep.tile([P, 2 * NBLK], F32, name="bias_sb")
        zt = keep.tile([P, 1], BF16, name="zt")
        nt = keep.tile([P, 1], BF16, name="nt")
        warm = keep.tile([P, 1], F32, name="warm")
        warm2 = keep.tile([P, 1], F32, name="warm2")
        sz = keep.tile([P, 1], F32, name="sz")
        sn = keep.tile([P, 1], F32, name="sn")
        nsz = keep.tile([P, 1], F32, name="nsz")
        amix = keep.tile([P, 1], F32, name="amix")
        zeros = keep.tile([P, B], BF16, name="zeros")
        bgB = keep.tile([P, CHUNK], F32, name="bgB")
        buB = keep.tile([P, CHUNK], F32, name="buB")
        ones = keep.tile([P, P], BF16, name="ones")
        brow = keep.tile([P, 2, CHUNK], BF16, name="brow")

        nc.vector.memset(xs[0][:].bitcast(I32), 0)
        nc.vector.memset(ws[0][0][:].bitcast(I32), 0)
        nc.vector.memset(xs[1][:].bitcast(I32), 0)
        nc.vector.memset(ws[1][0][:].bitcast(I32), 0)
        nc.vector.memset(warm[:], 0.0)
        nc.vector.memset(zeros[:], 0.0)
        nc.vector.memset(braw[64:128, :], 0.0)
        nc.vector.memset(ones[:], 1.0)
        nc.vector.memset(brow[:], 0.0)
        for i in (1, 2):
            for a in range(2):
                nc.vector.memset(ws[a][i][:].bitcast(I32), 0)

        nc.gpsimd.dma_start(out=braw[0:32, :], in_=bias_gate.rearrange("o (j p) -> (o j) p", p=P))
        nc.gpsimd.dma_start(out=braw[32:64, :], in_=bias_update.rearrange("o (j p) -> (o j) p", p=P))
        make_identity(nc, ident_bf[:])
        nc.gpsimd.dma_start(out=zt[:], in_=zeta.rearrange("a b -> (a b)").partition_broadcast(P))
        nc.gpsimd.dma_start(out=nt[:], in_=nu.rearrange("a b -> (a b)").partition_broadcast(P))
        make_identity(nc, ident_f[:])
        nc.gpsimd.dma_start(out=brow[0:1, 0, :], in_=bias_gate[:, CHUNK * KB : CHUNK * (KB + 1)])
        nc.gpsimd.dma_start(out=brow[0:1, 1, :], in_=bias_update[:, CHUNK * KB : CHUNK * (KB + 1)])

        nc.scalar.activation(out=warm2[:], in_=warm[:], func=ACT.Sigmoid)

        def load_scales(plane, dram, c0, c1):
            for quad in range(4):
                nc.sync.dma_start(
                    out=plane[32 * quad : 32 * quad + 4, :, :].bitcast(I32),
                    in_=dram[:, 4 * quad : 4 * quad + 4, c0:c1].rearrange("g r n -> r g n").bitcast(I32),
                )

        def load_codes(tile_ap, dram, b0, b1):
            nc.sync.dma_start(
                out=tile_ap[:].bitcast(I32), in_=dram[:, :, b0:b1].rearrange("g p n -> p g n").bitcast(I32)
            )

        def load_state(k):
            nc.sync.dma_start(out=st[k][:], in_=state_v[:, :, CHUNK * k : CHUNK * (k + 1)])

        for a in range(2):
            load_scales(xs[a], x_scales[a], 0, B)
            load_scales(ws[a][0], w_scales[a], 0, SC_RANGES[0][1])
            load_codes(xc[a], x_words[a], 0, 2 * B)
            load_codes(wc[a][0], w_words[a], 0, 2 * CHUNK)
        load_state(0)
        for item in LOAD_ORDER:
            if item < 0:
                i = -item
                for a in range(2):
                    load_scales(ws[a][i], w_scales[a], SC_RANGES[i][0], SC_RANGES[i][1])
            else:
                for a in range(2):
                    load_codes(wc[a][item], w_words[a], 2 * CHUNK * item, 2 * CHUNK * (item + 1))
                load_state(item)

        for i in range(WARM):
            dummy = psum.tile([P, B], F32, tag="oT", bufs=2, name="dummy")
            nc.tensor.matmul(out=dummy[:], lhsT=zeros[:, 0:P], rhs=zeros[:], start=True, stop=True)

        def scale_plane(a, j):
            ch = P * j
            for i, (c0, c1) in enumerate(SC_RANGES):
                if c0 <= ch < c1:
                    return ws[a][i], ch - c0
            raise ValueError("no range")

        pres = {}
        sts = {}
        cs = {}
        zs = {}
        outs = {}
        oTs = {}

        def mx_block(j, passes):
            k, jl = j // 4, j % 4
            if j not in pres:
                pres[j] = psum.tile([P, B], F32, tag="pre", bufs=4, name="pre")
            for q in passes:
                a, g = q // 2, q % 2
                plane, col = scale_plane(a, j)
                nc.tensor.matmul_mx(
                    out=pres[j][:],
                    lhsT=wc[a][k][:, g, 2 * P * jl : 2 * P * (jl + 1)].bitcast(FP4X4),
                    lhsT_scale=plane[:, g, col : col + P],
                    rhs=xc[a][:, g, :].bitcast(FP4X4),
                    rhs_scale=xs[a][:, g, :],
                    start=(q == 0),
                    stop=(q == 3),
                )

        def state_t(u):
            kind, j0, nb = UNITS[u]
            stT = psum.tile([P, nb, B], BF16, tag="stT", bufs=2, name="stT")
            for jj in range(nb):
                k, jl = (j0 + jj) // 4, (j0 + jj) % 4
                for bb in range(NBB):
                    nc.tensor.transpose(
                        stT[:, jj, P * bb : P * (bb + 1)], st[k][:, bb, P * jl : P * (jl + 1)], ident_bf[:]
                    )
            sts[u] = stT

        def act(u):
            kind, j0, nb = UNITS[u]
            c = work.tile([P, nb, B], F32, tag="c", name="c")
            z = work.tile([P, nb, B], F32, tag="z", name="z")
            for jj in range(nb):
                j = j0 + jj
                nc.scalar.activation(
                    out=c[:, jj, :], in_=pres[j][:], func=ACT.Tanh, bias=bias_sb[:, NBLK + j : NBLK + j + 1]
                )
            for jj in range(nb):
                j = j0 + jj
                nc.scalar.activation(out=z[:, jj, :], in_=pres[j][:], func=ACT.Sigmoid, bias=bias_sb[:, j : j + 1])
            cs[u] = c
            zs[u] = z

        t1s = {}
        t2s = {}

        def v3(u):
            kind, j0, nb = UNITS[u]
            t1s[u] = work.tile([P, nb, B], F32, tag="t1", name="t1")
            nc.vector.scalar_tensor_tensor(
                out=t1s[u][:], in0=cs[u][:], scalar=nsz[:, 0:1], in1=sts[u][:], op0=ALU.mult, op1=ALU.add
            )

        def v4(u):
            kind, j0, nb = UNITS[u]
            t2s[u] = work.tile([P, nb, B], F32, tag="t2", name="t2")
            nc.vector.tensor_tensor(out=t2s[u][:], in0=t1s[u][:], in1=zs[u][:], op=ALU.mult)

        def v5(u):
            kind, j0, nb = UNITS[u]
            outs[u] = work.tile([P, nb, B], F32, tag="o", bufs=4, name="o")
            nc.vector.scalar_tensor_tensor(
                out=outs[u][:], in0=cs[u][:], scalar=amix[:, 0:1], in1=t2s[u][:], op0=ALU.mult, op1=ALU.add
            )

        def out_t(u):
            kind, j0, nb = UNITS[u]
            halves = []
            for h in range(2):
                oT = psum.tile([P, 2, nb * P], F32, tag="oT", bufs=2, name="oT")
                for b2 in range(2):
                    bb = 2 * h + b2
                    for jj in range(nb):
                        nc.tensor.transpose(
                            oT[:, b2, P * jj : P * (jj + 1)], outs[u][:, jj, P * bb : P * (bb + 1)], ident_f[:]
                        )
                halves.append(oT)
            oTs[u] = halves

        def evac(u):
            kind, j0, nb = UNITS[u]
            osb = work.tile([P, NBB, nb * P], F32, tag="osb", bufs=4, name="osb")
            for h in range(2):
                if h == 1 and u in V_EVAC:
                    nc.vector.tensor_copy(out=osb[:, 2 * h : 2 * h + 2, :], in_=oTs[u][h][:])
                else:
                    nc.scalar.copy(out=osb[:, 2 * h : 2 * h + 2, :], in_=oTs[u][h][:])
            nc.sync.dma_start(out=out_v[:, :, P * j0 : P * (j0 + nb)], in_=osb[:])

        avs = {}
        bvs = {}

        def mx_b(u):
            bb = u
            pre = psum.tile([P, CHUNK], F32, tag="pre", bufs=4, name="pre")
            for q in range(4):
                a, g = q // 2, q % 2
                plane, col = scale_plane(a, 4 * KB)
                nc.tensor.matmul_mx(
                    out=pre[:],
                    lhsT=xc[a][:, g, 2 * P * bb : 2 * P * (bb + 1)].bitcast(FP4X4),
                    lhsT_scale=xs[a][:, g, P * bb : P * (bb + 1)],
                    rhs=wc[a][KB][:, g, :].bitcast(FP4X4),
                    rhs_scale=plane[:, g, col : col + CHUNK],
                    start=(q == 0),
                    stop=(q == 3),
                )
            pres[("B", bb)] = pre

        def v12_b(u):
            bb = u
            avs[("B", u)] = work.tile([P, CHUNK], F32, tag="av", bufs=2, name="av")
            bvs[("B", u)] = work.tile([P, CHUNK], F32, tag="bv", bufs=2, name="bv")
            nc.vector.tensor_tensor(out=bvs[("B", u)][:], in0=pres[("B", bb)][:], in1=buB[:], op=ALU.add)
            nc.vector.tensor_tensor(out=avs[("B", u)][:], in0=pres[("B", bb)][:], in1=bgB[:], op=ALU.add)

        def act_b(u):
            cs[("B", u)] = work.tile([P, CHUNK], F32, tag="cB", bufs=2, name="cB")
            zs[("B", u)] = work.tile([P, CHUNK], F32, tag="zB", bufs=2, name="zB")
            nc.scalar.activation(out=cs[("B", u)][:], in_=bvs[("B", u)][:], func=ACT.Tanh)
            nc.scalar.activation(out=zs[("B", u)][:], in_=avs[("B", u)][:], func=ACT.Sigmoid)

        def v3_b(u):
            bb = u
            t1s[("B", u)] = work.tile([P, CHUNK], F32, tag="t1B", bufs=2, name="t1B")
            nc.vector.scalar_tensor_tensor(
                out=t1s[("B", u)][:], in0=cs[("B", u)][:], scalar=nsz[:, 0:1], in1=st[KB][:, bb, :], op0=ALU.mult, op1=ALU.add
            )

        def v4_b(u):
            t2s[("B", u)] = work.tile([P, CHUNK], F32, tag="t2B", bufs=2, name="t2B")
            nc.vector.tensor_tensor(out=t2s[("B", u)][:], in0=t1s[("B", u)][:], in1=zs[("B", u)][:], op=ALU.mult)

        def v5_b(u):
            bb = u
            ob = work.tile([P, CHUNK], F32, tag="ob", bufs=2, name="ob")
            nc.vector.scalar_tensor_tensor(
                out=ob[:], in0=cs[("B", u)][:], scalar=amix[:, 0:1], in1=t2s[("B", u)][:], op0=ALU.mult, op1=ALU.add
            )
            nc.sync.dma_start(out=out[P * bb : P * (bb + 1), CHUNK * KB : CHUNK * (KB + 1)], in_=ob[:])

        def kind_of(u):
            if 0 <= u < NU:
                return UNITS[u][0]
            return "-"

        for j in range(4):
            mx_block(j, (0, 1))
        bT = psum.tile([P, P], BF16, tag="stT", bufs=2, name="bT")
        nc.tensor.transpose(bT[:], braw[:], ident_bf[:])
        nc.vector.tensor_copy(out=bias_sb[:], in_=bT[:, 0 : 2 * NBLK])
        nc.scalar.activation(out=sz[:], in_=zt[:], func=ACT.Sigmoid)
        nc.scalar.activation(out=sn[:], in_=nt[:], func=ACT.Sigmoid)
        nc.vector.tensor_scalar_mul(out=nsz[:], in0=sz[:], scalar1=-1.0)
        nc.vector.tensor_add(out=amix[:], in0=sz[:], in1=sn[:])
        for j in range(4):
            mx_block(j, (2, 3))

        def b_at(s, lag):
            return B_AT.get(s - lag, None)

        for s in range(NU + 4):
            k0, k1, k2 = kind_of(s), kind_of(s - 1), kind_of(s - 2)
            if k0 == "A":
                kind, j0, nb = UNITS[s]
                if j0 >= 4:
                    for jj in range(nb):
                        mx_block(j0 + jj, (0, 1, 2, 3))
            if b_at(s, 0) is not None:
                mx_b(b_at(s, 0))
            if k0 == "A":
                state_t(s)
            if k2 == "A":
                out_t(s - 2)
            if k0 == "A":
                act(s)
            if k2 == "A":
                evac(s - 2)
            if s == 1:
                for i, dst in enumerate((bgB, buB)):
                    pb = psum.tile([P, CHUNK], F32, tag="oT", bufs=2, name="pb")
                    nc.tensor.matmul(out=pb[:], lhsT=ones[:], rhs=brow[:, i, :], start=True, stop=True)
                    nc.scalar.copy(out=dst[:], in_=pb[:])
            if b_at(s, 1) is not None:
                act_b(b_at(s, 1))
            if k0 == "A":
                v3(s)
            if b_at(s, 2) is not None:
                v3_b(b_at(s, 2))
            if k1 == "A":
                v5(s - 1)
            if b_at(s, 3) is not None:
                v5_b(b_at(s, 3))
            if k0 == "A":
                v4(s)
            if b_at(s, 2) is not None:
                v4_b(b_at(s, 2))
            if b_at(s, 0) is not None:
                v12_b(b_at(s, 0))
